import numpy as np
import ml_dtypes


def mxq(x, axis, fmt="e4m3"):
    dtype, down = {"e4m3": (ml_dtypes.float8_e4m3fn, 7), "e5m2": (ml_dtypes.float8_e5m2, 14)}[fmt]
    v = np.moveaxis(np.asarray(x, np.float32).astype(ml_dtypes.bfloat16).astype(np.float64), axis, -1)
    blocks = v.reshape(v.shape[:-1] + (-1, 32))
    amax = np.abs(blocks).max(-1, keepdims=True)
    byte = np.maximum(np.where(amax > 0, np.frexp(amax)[1] - 1 + 127, 0) - down, 1)
    scale = np.exp2(byte - 127.0)
    codes = (blocks / scale).astype(np.float32).astype(dtype).astype(np.float64)
    return np.moveaxis((codes * scale).reshape(v.shape), -1, axis)


WIDE = False


def mx_kscale(k):
    if not WIDE:
        return np.ones(k)
    levels = np.array([10, -10, 5, -5, 0])
    a = np.random.permutation(np.resize(levels, k // 512 * 4)).reshape(k // 512, 4)
    idx = np.arange(k)
    return np.exp2(a[idx // 512, idx % 128 // 32])


BF16 = ml_dtypes.bfloat16


def bf(x):
    return np.asarray(x, np.float32).astype(BF16)


def f64(x):
    return np.asarray(x).astype(np.float64)


N, F, K, D, E = 128, 512, 512, 512, 512
SIG = 2.0
PS = 16.0


def setup_inputs():
    t, sx = mx_kscale(K), mx_kscale(F)
    s = np.concatenate([sx, np.ones(E)])
    g = SIG * np.random.standard_normal((N, K))
    e = np.exp(g - g.max(-1, keepdims=True))
    w = e / e.sum(-1, keepdims=True) * (np.random.uniform(size=K) * PS)[None, :]
    return {"att_prior": bf(w * t[None, :]),
            "dic": bf(np.random.standard_normal((K, D)) / t[:, None]),
            "x": bf(np.random.standard_normal((N, F)) * sx[None, :]),
            "cs_w": bf(np.random.standard_normal((K, F + E)) * (F + E) ** -0.5 / s[None, :]),
            "cs_b": bf(np.random.standard_normal(K) * 0.1)}


def reference(att_prior, dic, x, cs_w, cs_b):
    z = mxq(f64(att_prior), 1, "e4m3") @ mxq(f64(dic), 0, "e4m3")
    xz = np.concatenate([f64(x), z], axis=1)
    causal_logits = (mxq(xz, 1, "e4m3") @ mxq(f64(cs_w), 1, "e4m3").T) + f64(cs_b)
    return causal_logits, z

@@ -1,0 +1,185 @@
+from contextlib import ExitStack
+
+import concourse.mybir as mybir
+from concourse.masks import make_identity
+
+BF16 = mybir.dt.bfloat16
+F32 = mybir.dt.float32
+U32 = mybir.dt.uint32
+U8 = mybir.dt.uint8
+FP8X4 = mybir.dt.float8_e4m3fn_x4
+
+P = 128
+PACK = 4
+K_PASS = P * PACK
+WORDS = K_PASS // 2
+D = 512
+OUT = 512
+W_PASSES = 2
+GROUPS = D // P
+OUT_CHUNKS = OUT // P
+VECTOR_GROUPS = 3
+
+FLOPS = 2 * P * K_PASS * D + 2 * P * (W_PASSES * K_PASS) * OUT
+
+
+def tile_visualdeconfounder_pb_s_kernel(tc, att_prior, dic, x, cs_w, cs_b, out_0, out_1):
+    nc = tc.nc
+    with ExitStack() as ctx:
+        keep = ctx.enter_context(tc.tile_pool(name="keep", bufs=1))
+        turned = ctx.enter_context(tc.psum_pool(name="turned", bufs=4))
+        sums = ctx.enter_context(tc.psum_pool(name="sums", bufs=1))
+        ctx.enter_context(tc.manual_schedule())
+
+        ident = keep.tile([P, P], F32)
+        make_identity(nc, ident[:])
+        ones = keep.tile([P, P], BF16)
+        nc.vector.memset(ones[:], 1.0)
+        bias_rows = keep.tile([P, OUT], BF16)
+        nc.vector.memset(bias_rows[:], 0.0)
+
+        nc.scalar.dma_start(out=bias_rows[0:1, :], in_=cs_b.unsqueeze(0))
+        dic_raw = keep.tile([P, PACK, D], BF16)
+        nc.sync.dma_start(
+            out=dic_raw[:].rearrange("p (u e) c -> p u e c", u=2),
+            in_=dic.rearrange("(u p e) c -> p u e c", u=2, e=2),
+        )
+        ax_sb = keep.tile([P, 2, K_PASS], BF16)
+        nc.sync.dma_start(out=ax_sb[:, 0, :], in_=att_prior)
+        nc.sync.dma_start(out=ax_sb[:, 1, :], in_=x)
+        w_sb = keep.tile([P, OUT_CHUNKS, W_PASSES * K_PASS], BF16)
+        for oc in range(OUT_CHUNKS):
+            nc.sync.dma_start(out=w_sb[:, oc, :], in_=cs_w[oc * P : (oc + 1) * P, :])
+
+        dic_grouped = keep.tile([P, D, PACK], BF16, align_bytes=64)
+        dic_sorted = dic_raw[:].rearrange("p t (u q e) -> p u e q t", u=2, e=2)
+        for j in range(GROUPS):
+            engine_copy = nc.vector.tensor_copy if j < VECTOR_GROUPS else nc.scalar.copy
+            engine_copy(out=dic_grouped[:, j * P : (j + 1) * P, :], in_=dic_sorted[:, j // 2, j % 2])
+
+        ax_words = ax_sb[:].bitcast(F32)
+        ax_t = turned.tile([P, 2 * 2, P], F32, tag="turned")
+        for s in range(2):
+            for u in range(2):
+                nc.tensor.transpose(ax_t[:, 2 * s + u, :], ax_words[:, s, u * P : (u + 1) * P], ident[:])
+        ax_grouped = keep.tile([P, 2, P, PACK], BF16, align_bytes=64)
+        nc.scalar.copy(out=ax_grouped[:].bitcast(F32), in_=ax_t[:].rearrange("p (s u) n -> p s n u", s=2))
+
+        bias_ps = sums.tile([P, OUT], F32)
+        nc.tensor.matmul(out=bias_ps[:], lhsT=ones[:], rhs=bias_rows[:], start=True, stop=True)
+
+        dic_codes = keep.tile([P, D], U32, align_bytes=64)
+        dic_scales = keep.tile([P, D], U8, align_bytes=64)
+        for j in range(GROUPS):
+            cols = slice(j * P, (j + 1) * P)
+            nc.vector.quantize_mx(
+                out=dic_codes[:, cols].bitcast(FP8X4),
+                scales=dic_scales[:, cols],
+                in_=dic_grouped[:, cols, :].rearrange("p c t -> p (c t)"),
+            )
+        ax_codes = keep.tile([P, 2 * P], U32, align_bytes=64)
+        ax_scales = keep.tile([P, 2 * P], U8, align_bytes=64)
+        nc.vector.quantize_mx(
+            out=ax_codes[:].bitcast(FP8X4),
+            scales=ax_scales[:],
+            in_=ax_grouped[:].rearrange("p s n t -> p (s n t)"),
+        )
+        att_cols = slice(0, P)
+        x_cols = slice(P, 2 * P)
+
+        w_words = w_sb[:].bitcast(F32)
+        w_grouped = keep.tile([P, W_PASSES, OUT, PACK], BF16, align_bytes=64)
+        w_codes = keep.tile([P, W_PASSES, OUT], U32, align_bytes=64)
+        w_scales = keep.tile([P, W_PASSES, OUT], U8, align_bytes=64)
+
+        def turn_w(oc):
+            w_t = turned.tile([P, W_PASSES * 2, P], F32, tag="turned")
+            for gu in range(W_PASSES * 2):
+                nc.tensor.transpose(w_t[:, gu, :], w_words[:, oc, gu * P : (gu + 1) * P], ident[:])
+            nc.scalar.copy(
+                out=w_grouped[:, :, oc * P : (oc + 1) * P, :].bitcast(F32),
+                in_=w_t[:].rearrange("p (g u) o -> p g o u", g=W_PASSES),
+            )
+
+        def quantise_w(oc):
+            rows = slice(oc * P, (oc + 1) * P)
+            for g in range(W_PASSES):
+                nc.vector.quantize_mx(
+                    out=w_codes[:, g, rows].bitcast(FP8X4),
+                    scales=w_scales[:, g, rows],
+                    in_=w_grouped[:, g, rows, :].rearrange("p o t -> p (o t)"),
+                )
+
+        turn_w(0)
+        turn_w(1)
+
+        zt_ps = sums.tile([P, GROUPS, P], F32)
+        for j in range(GROUPS):
+            cols = slice(j * P, (j + 1) * P)
+            nc.tensor.matmul_mx(
+                out=zt_ps[:, j, :],
+                lhsT=dic_codes[:, cols].bitcast(FP8X4),
+                lhsT_scale=dic_scales[:, cols],
+                rhs=ax_codes[:, att_cols].bitcast(FP8X4),
+                rhs_scale=ax_scales[:, att_cols],
+                start=True,
+                stop=True,
+            )
+        quantise_w(0)
+        z_grouped = keep.tile([P, P, PACK], BF16, align_bytes=64)
+        nc.vector.tensor_copy(out=z_grouped[:], in_=zt_ps[:].rearrange("q j n -> q n j"))
+        quantise_w(1)
+        z_codes = keep.tile([P, P], U32, align_bytes=64)
+        z_scales = keep.tile([P, P], U8, align_bytes=64)
+        nc.vector.quantize_mx(
+            out=z_codes[:].bitcast(FP8X4),
+            scales=z_scales[:],
+            in_=z_grouped[:].rearrange("q n t -> q (n t)"),
+        )
+
+        turn_w(2)
+        turn_w(3)
+        quantise_w(2)
+        quantise_w(3)
+        bias_sb = keep.tile([P, OUT], F32)
+        nc.scalar.copy(out=bias_sb[:], in_=bias_ps[:])
+
+        z_ps = sums.tile([P, D], F32)
+        nc.tensor.matmul_mx(
+            out=z_ps[:],
+            lhsT=ax_codes[:, att_cols].bitcast(FP8X4),
+            lhsT_scale=ax_scales[:, att_cols],
+            rhs=dic_codes[:].bitcast(FP8X4),
+            rhs_scale=dic_scales[:],
+            start=True,
+            stop=True,
+        )
+        z_sb = keep.tile([P, D], F32)
+        nc.scalar.copy(
+            out=z_sb[:].rearrange("n (u q e) -> n u q e", u=2, e=2),
+            in_=z_ps[:].rearrange("n (u e q) -> n u q e", u=2, e=2),
+        )
+        nc.sync.dma_start(out=out_1, in_=z_sb[:])
+
+        logits_ps = sums.tile([P, OUT], F32)
+        nc.tensor.matmul_mx(
+            out=logits_ps[:],
+            lhsT=ax_codes[:, x_cols].bitcast(FP8X4),
+            lhsT_scale=ax_scales[:, x_cols],
+            rhs=w_codes[:, 0, :].bitcast(FP8X4),
+            rhs_scale=w_scales[:, 0, :],
+            start=True,
+            stop=False,
+        )
+        nc.tensor.matmul_mx(
+            out=logits_ps[:],
+            lhsT=z_codes[:].bitcast(FP8X4),
+            lhsT_scale=z_scales[:],
+            rhs=w_codes[:, 1, :].bitcast(FP8X4),
+            rhs_scale=w_scales[:, 1, :],
+            start=False,
+            stop=True,
+        )
+        logits_sb = keep.tile([P, OUT], F32)
+        nc.vector.tensor_tensor(out=logits_sb[:], in0=logits_ps[:], in1=bias_sb[:], op=mybir.AluOpType.add)
+        nc.sync.dma_start(out=out_0, in_=logits_sb[:])

@@ -27,8 +27,9 @@ def tile_visualdeconfounder_pb_s_kernel(tc, att_prior, dic, x, cs_w, cs_b, out_0
     nc = tc.nc
     with ExitStack() as ctx:
         keep = ctx.enter_context(tc.tile_pool(name="keep", bufs=1))
-        turned = ctx.enter_context(tc.psum_pool(name="turned", bufs=4))
+        turned = ctx.enter_context(tc.psum_pool(name="turned", bufs=3))
         sums = ctx.enter_context(tc.psum_pool(name="sums", bufs=1))
+        finished = ctx.enter_context(tc.psum_pool(name="finished", bufs=2))
         ctx.enter_context(tc.manual_schedule())
 
         ident = keep.tile([P, P], F32)
@@ -51,6 +52,11 @@ def tile_visualdeconfounder_pb_s_kernel(tc, att_prior, dic, x, cs_w, cs_b, out_0
         for oc in range(OUT_CHUNKS):
             nc.sync.dma_start(out=w_sb[:, oc, :], in_=cs_w[oc * P : (oc + 1) * P, :])
 
+        bias_ps = sums.tile([P, OUT], BF16)
+        nc.tensor.matmul(out=bias_ps[:], lhsT=ones[:], rhs=bias_rows[:], start=True, stop=True)
+        bias_sb = keep.tile([P, OUT], BF16)
+        nc.scalar.copy(out=bias_sb[:], in_=bias_ps[:])
+
         dic_grouped = keep.tile([P, D, PACK], BF16, align_bytes=64)
         dic_sorted = dic_raw[:].rearrange("p t (u q e) -> p u e q t", u=2, e=2)
         for j in range(GROUPS):
@@ -64,9 +70,6 @@ def tile_visualdeconfounder_pb_s_kernel(tc, att_prior, dic, x, cs_w, cs_b, out_0
                 nc.tensor.transpose(ax_t[:, 2 * s + u, :], ax_words[:, s, u * P : (u + 1) * P], ident[:])
         ax_grouped = keep.tile([P, 2, P, PACK], BF16, align_bytes=64)
         nc.scalar.copy(out=ax_grouped[:].bitcast(F32), in_=ax_t[:].rearrange("p (s u) n -> p s n u", s=2))
-
-        bias_ps = sums.tile([P, OUT], F32)
-        nc.tensor.matmul(out=bias_ps[:], lhsT=ones[:], rhs=bias_rows[:], start=True, stop=True)
 
         dic_codes = keep.tile([P, D], U32, align_bytes=64)
         dic_scales = keep.tile([P, D], U8, align_bytes=64)
@@ -141,8 +144,6 @@ def tile_visualdeconfounder_pb_s_kernel(tc, att_prior, dic, x, cs_w, cs_b, out_0
         turn_w(3)
         quantise_w(2)
         quantise_w(3)
-        bias_sb = keep.tile([P, OUT], F32)
-        nc.scalar.copy(out=bias_sb[:], in_=bias_ps[:])
 
         z_ps = sums.tile([P, D], F32)
         nc.tensor.matmul_mx(
@@ -161,25 +162,29 @@ def tile_visualdeconfounder_pb_s_kernel(tc, att_prior, dic, x, cs_w, cs_b, out_0
         )
         nc.sync.dma_start(out=out_1, in_=z_sb[:])
 
-        logits_ps = sums.tile([P, OUT], F32)
-        nc.tensor.matmul_mx(
-            out=logits_ps[:],
-            lhsT=ax_codes[:, x_cols].bitcast(FP8X4),
-            lhsT_scale=ax_scales[:, x_cols],
-            rhs=w_codes[:, 0, :].bitcast(FP8X4),
-            rhs_scale=w_scales[:, 0, :],
-            start=True,
-            stop=False,
-        )
-        nc.tensor.matmul_mx(
-            out=logits_ps[:],
-            lhsT=z_codes[:].bitcast(FP8X4),
-            lhsT_scale=z_scales[:],
-            rhs=w_codes[:, 1, :].bitcast(FP8X4),
-            rhs_scale=w_scales[:, 1, :],
-            start=False,
-            stop=True,
-        )
         logits_sb = keep.tile([P, OUT], F32)
-        nc.vector.tensor_tensor(out=logits_sb[:], in0=logits_ps[:], in1=bias_sb[:], op=mybir.AluOpType.add)
-        nc.sync.dma_start(out=out_0, in_=logits_sb[:])
+        for oc in range(OUT_CHUNKS):
+            rows = slice(oc * P, (oc + 1) * P)
+            logits_ps = finished.tile([P, P], F32)
+            nc.tensor.matmul_mx(
+                out=logits_ps[:],
+                lhsT=ax_codes[:, x_cols].bitcast(FP8X4),
+                lhsT_scale=ax_scales[:, x_cols],
+                rhs=w_codes[:, 0, rows].bitcast(FP8X4),
+                rhs_scale=w_scales[:, 0, rows],
+                start=True,
+                stop=False,
+            )
+            nc.tensor.matmul_mx(
+                out=logits_ps[:],
+                lhsT=z_codes[:].bitcast(FP8X4),
+                lhsT_scale=z_scales[:],
+                rhs=w_codes[:, 1, rows].bitcast(FP8X4),
+                rhs_scale=w_scales[:, 1, rows],
+                start=False,
+                stop=True,
+            )
+            nc.vector.tensor_tensor(
+                out=logits_sb[:, rows], in0=logits_ps[:], in1=bias_sb[:, rows], op=mybir.AluOpType.add
+            )
+            nc.sync.dma_start(out=out_0[:, rows], in_=logits_sb[:, rows])

@@ -52,11 +52,6 @@ def tile_visualdeconfounder_pb_s_kernel(tc, att_prior, dic, x, cs_w, cs_b, out_0
         for oc in range(OUT_CHUNKS):
             nc.sync.dma_start(out=w_sb[:, oc, :], in_=cs_w[oc * P : (oc + 1) * P, :])
 
-        bias_ps = sums.tile([P, OUT], BF16)
-        nc.tensor.matmul(out=bias_ps[:], lhsT=ones[:], rhs=bias_rows[:], start=True, stop=True)
-        bias_sb = keep.tile([P, OUT], BF16)
-        nc.scalar.copy(out=bias_sb[:], in_=bias_ps[:])
-
         dic_grouped = keep.tile([P, D, PACK], BF16, align_bytes=64)
         dic_sorted = dic_raw[:].rearrange("p t (u q e) -> p u e q t", u=2, e=2)
         for j in range(GROUPS):
@@ -128,6 +123,9 @@ def tile_visualdeconfounder_pb_s_kernel(tc, att_prior, dic, x, cs_w, cs_b, out_0
                 start=True,
                 stop=True,
             )
+        bias_ps = sums.tile([P, OUT], BF16)
+        nc.tensor.matmul(out=bias_ps[:], lhsT=ones[:], rhs=bias_rows[:], start=True, stop=True)
+
         quantise_w(0)
         z_grouped = keep.tile([P, P, PACK], BF16, align_bytes=64)
         nc.vector.tensor_copy(out=z_grouped[:], in_=zt_ps[:].rearrange("q j n -> q n j"))
@@ -142,6 +140,8 @@ def tile_visualdeconfounder_pb_s_kernel(tc, att_prior, dic, x, cs_w, cs_b, out_0
 
         turn_w(2)
         turn_w(3)
+        bias_sb = keep.tile([P, OUT], BF16)
+        nc.scalar.copy(out=bias_sb[:], in_=bias_ps[:])
         quantise_w(2)
         quantise_w(3)
 

@@ -19,6 +19,7 @@ W_PASSES = 2
 GROUPS = D // P
 OUT_CHUNKS = OUT // P
 VECTOR_GROUPS = 3
+WARM_PASSES = 24
 
 FLOPS = 2 * P * K_PASS * D + 2 * P * (W_PASSES * K_PASS) * OUT
 
@@ -31,6 +32,23 @@ def tile_visualdeconfounder_pb_s_kernel(tc, att_prior, dic, x, cs_w, cs_b, out_0
         sums = ctx.enter_context(tc.psum_pool(name="sums", bufs=1))
         finished = ctx.enter_context(tc.psum_pool(name="finished", bufs=2))
         ctx.enter_context(tc.manual_schedule())
+
+        idle_values = keep.tile([P, K_PASS], BF16, align_bytes=64)
+        nc.vector.memset(idle_values[:], 0.0)
+        idle_codes = keep.tile([P, P], U32, align_bytes=64)
+        idle_scales = keep.tile([P, P], U8, align_bytes=64)
+        nc.vector.quantize_mx(out=idle_codes[:].bitcast(FP8X4), scales=idle_scales[:], in_=idle_values[:])
+        idle_ps = turned.tile([P, P], F32, tag="turned")
+        for i in range(WARM_PASSES):
+            nc.tensor.matmul_mx(
+                out=idle_ps[:],
+                lhsT=idle_codes[:].bitcast(FP8X4),
+                lhsT_scale=idle_scales[:],
+                rhs=idle_codes[:].bitcast(FP8X4),
+                rhs_scale=idle_scales[:],
+                start=True,
+                stop=True,
+            )
 
         ident = keep.tile([P, P], F32)
         make_identity(nc, ident[:])

@@ -12,14 +12,12 @@ FP8X4 = mybir.dt.float8_e4m3fn_x4
 P = 128
 PACK = 4
 K_PASS = P * PACK
-WORDS = K_PASS // 2
 D = 512
 OUT = 512
 W_PASSES = 2
 GROUPS = D // P
 OUT_CHUNKS = OUT // P
 VECTOR_GROUPS = 3
-WARM_PASSES = 24
 
 FLOPS = 2 * P * K_PASS * D + 2 * P * (W_PASSES * K_PASS) * OUT
 
@@ -33,42 +31,39 @@ def tile_visualdeconfounder_pb_s_kernel(tc, att_prior, dic, x, cs_w, cs_b, out_0
         finished = ctx.enter_context(tc.psum_pool(name="finished", bufs=2))
         ctx.enter_context(tc.manual_schedule())
 
-        idle_values = keep.tile([P, K_PASS], BF16, align_bytes=64)
-        nc.vector.memset(idle_values[:], 0.0)
-        idle_codes = keep.tile([P, P], U32, align_bytes=64)
-        idle_scales = keep.tile([P, P], U8, align_bytes=64)
-        nc.vector.quantize_mx(out=idle_codes[:].bitcast(FP8X4), scales=idle_scales[:], in_=idle_values[:])
-        idle_ps = turned.tile([P, P], F32, tag="turned")
-        for i in range(WARM_PASSES):
-            nc.tensor.matmul_mx(
-                out=idle_ps[:],
-                lhsT=idle_codes[:].bitcast(FP8X4),
-                lhsT_scale=idle_scales[:],
-                rhs=idle_codes[:].bitcast(FP8X4),
-                rhs_scale=idle_scales[:],
-                start=True,
-                stop=True,
-            )
-
         ident = keep.tile([P, P], F32)
         make_identity(nc, ident[:])
-        ones = keep.tile([P, P], BF16)
-        nc.vector.memset(ones[:], 1.0)
         bias_rows = keep.tile([P, OUT], BF16)
         nc.vector.memset(bias_rows[:], 0.0)
+        ones = keep.tile([P, P], BF16)
+        nc.vector.memset(ones[:], 1.0)
 
-        nc.scalar.dma_start(out=bias_rows[0:1, :], in_=cs_b.unsqueeze(0))
         dic_raw = keep.tile([P, PACK, D], BF16)
         nc.sync.dma_start(
             out=dic_raw[:].rearrange("p (u e) c -> p u e c", u=2),
             in_=dic.rearrange("(u p e) c -> p u e c", u=2, e=2),
         )
-        ax_sb = keep.tile([P, 2, K_PASS], BF16)
-        nc.sync.dma_start(out=ax_sb[:, 0, :], in_=att_prior)
-        nc.sync.dma_start(out=ax_sb[:, 1, :], in_=x)
+        att_sb = keep.tile([P, K_PASS], BF16)
+        nc.sync.dma_start(out=att_sb[:], in_=att_prior)
+        x_sb = keep.tile([P, K_PASS], BF16)
+        nc.sync.dma_start(out=x_sb[:], in_=x)
+        nc.sync.dma_start(out=bias_rows[0:1, :], in_=cs_b.unsqueeze(0))
         w_sb = keep.tile([P, OUT_CHUNKS, W_PASSES * K_PASS], BF16)
         for oc in range(OUT_CHUNKS):
             nc.sync.dma_start(out=w_sb[:, oc, :], in_=cs_w[oc * P : (oc + 1) * P, :])
+
+        def turn(rows_sb, grouped):
+            passes = grouped.shape[1]
+            words = rows_sb.bitcast(F32)
+            words_t = turned.tile([P, passes * 2, P], F32, tag="turned")
+            for gu in range(passes * 2):
+                nc.tensor.transpose(words_t[:, gu, :], words[:, gu * P : (gu + 1) * P], ident[:])
+            nc.scalar.copy(out=grouped.bitcast(F32), in_=words_t[:].rearrange("p (g u) r -> p g r u", g=passes))
+
+        def quantise(grouped, codes, scales):
+            nc.vector.quantize_mx(
+                out=codes.bitcast(FP8X4), scales=scales, in_=grouped.rearrange("p c t -> p (c t)")
+            )
 
         dic_grouped = keep.tile([P, D, PACK], BF16, align_bytes=64)
         dic_sorted = dic_raw[:].rearrange("p t (u q e) -> p u e q t", u=2, e=2)
@@ -76,55 +71,33 @@ def tile_visualdeconfounder_pb_s_kernel(tc, att_prior, dic, x, cs_w, cs_b, out_0
             engine_copy = nc.vector.tensor_copy if j < VECTOR_GROUPS else nc.scalar.copy
             engine_copy(out=dic_grouped[:, j * P : (j + 1) * P, :], in_=dic_sorted[:, j // 2, j % 2])
 
-        ax_words = ax_sb[:].bitcast(F32)
-        ax_t = turned.tile([P, 2 * 2, P], F32, tag="turned")
-        for s in range(2):
-            for u in range(2):
-                nc.tensor.transpose(ax_t[:, 2 * s + u, :], ax_words[:, s, u * P : (u + 1) * P], ident[:])
-        ax_grouped = keep.tile([P, 2, P, PACK], BF16, align_bytes=64)
-        nc.scalar.copy(out=ax_grouped[:].bitcast(F32), in_=ax_t[:].rearrange("p (s u) n -> p s n u", s=2))
+        att_grouped = keep.tile([P, 1, P, PACK], BF16, align_bytes=64)
+        turn(att_sb[:], att_grouped[:])
+        x_grouped = keep.tile([P, 1, P, PACK], BF16, align_bytes=64)
+        turn(x_sb[:], x_grouped[:])
 
         dic_codes = keep.tile([P, D], U32, align_bytes=64)
         dic_scales = keep.tile([P, D], U8, align_bytes=64)
         for j in range(GROUPS):
             cols = slice(j * P, (j + 1) * P)
-            nc.vector.quantize_mx(
-                out=dic_codes[:, cols].bitcast(FP8X4),
-                scales=dic_scales[:, cols],
-                in_=dic_grouped[:, cols, :].rearrange("p c t -> p (c t)"),
-            )
-        ax_codes = keep.tile([P, 2 * P], U32, align_bytes=64)
-        ax_scales = keep.tile([P, 2 * P], U8, align_bytes=64)
-        nc.vector.quantize_mx(
-            out=ax_codes[:].bitcast(FP8X4),
-            scales=ax_scales[:],
-            in_=ax_grouped[:].rearrange("p s n t -> p (s n t)"),
-        )
-        att_cols = slice(0, P)
-        x_cols = slice(P, 2 * P)
+            quantise(dic_grouped[:, cols, :], dic_codes[:, cols], dic_scales[:, cols])
+        att_codes = keep.tile([P, P], U32, align_bytes=64)
+        att_scales = keep.tile([P, P], U8, align_bytes=64)
+        quantise(att_grouped[:, 0], att_codes[:], att_scales[:])
 
-        w_words = w_sb[:].bitcast(F32)
-        w_grouped = keep.tile([P, W_PASSES, OUT, PACK], BF16, align_bytes=64)
-        w_codes = keep.tile([P, W_PASSES, OUT], U32, align_bytes=64)
-        w_scales = keep.tile([P, W_PASSES, OUT], U8, align_bytes=64)
+        w_grouped = keep.tile([P, OUT_CHUNKS, W_PASSES, P, PACK], BF16, align_bytes=64)
+        w_codes = keep.tile([P, OUT_CHUNKS, W_PASSES, P], U32, align_bytes=64)
+        w_scales = keep.tile([P, OUT_CHUNKS, W_PASSES, P], U8, align_bytes=64)
 
         def turn_w(oc):
-            w_t = turned.tile([P, W_PASSES * 2, P], F32, tag="turned")
-            for gu in range(W_PASSES * 2):
-                nc.tensor.transpose(w_t[:, gu, :], w_words[:, oc, gu * P : (gu + 1) * P], ident[:])
-            nc.scalar.copy(
-                out=w_grouped[:, :, oc * P : (oc + 1) * P, :].bitcast(F32),
-                in_=w_t[:].rearrange("p (g u) o -> p g o u", g=W_PASSES),
-            )
+            turn(w_sb[:, oc, :], w_grouped[:, oc])
 
         def quantise_w(oc):
-            rows = slice(oc * P, (oc + 1) * P)
-            for g in range(W_PASSES):
-                nc.vector.quantize_mx(
-                    out=w_codes[:, g, rows].bitcast(FP8X4),
-                    scales=w_scales[:, g, rows],
-                    in_=w_grouped[:, g, rows, :].rearrange("p o t -> p (o t)"),
-                )
+            quantise(
+                w_grouped[:, oc].rearrange("p g o t -> p (g o) t"),
+                w_codes[:, oc].rearrange("p g o -> p (g o)"),
+                w_scales[:, oc].rearrange("p g o -> p (g o)"),
+            )
 
         turn_w(0)
         turn_w(1)
@@ -136,38 +109,39 @@ def tile_visualdeconfounder_pb_s_kernel(tc, att_prior, dic, x, cs_w, cs_b, out_0
                 out=zt_ps[:, j, :],
                 lhsT=dic_codes[:, cols].bitcast(FP8X4),
                 lhsT_scale=dic_scales[:, cols],
-                rhs=ax_codes[:, att_cols].bitcast(FP8X4),
-                rhs_scale=ax_scales[:, att_cols],
+                rhs=att_codes[:].bitcast(FP8X4),
+                rhs_scale=att_scales[:],
                 start=True,
                 stop=True,
             )
-        bias_ps = sums.tile([P, OUT], BF16)
-        nc.tensor.matmul(out=bias_ps[:], lhsT=ones[:], rhs=bias_rows[:], start=True, stop=True)
 
-        quantise_w(0)
+        x_codes = keep.tile([P, P], U32, align_bytes=64)
+        x_scales = keep.tile([P, P], U8, align_bytes=64)
+        quantise(x_grouped[:, 0], x_codes[:], x_scales[:])
         z_grouped = keep.tile([P, P, PACK], BF16, align_bytes=64)
         nc.vector.tensor_copy(out=z_grouped[:], in_=zt_ps[:].rearrange("q j n -> q n j"))
-        quantise_w(1)
+        quantise_w(0)
         z_codes = keep.tile([P, P], U32, align_bytes=64)
         z_scales = keep.tile([P, P], U8, align_bytes=64)
-        nc.vector.quantize_mx(
-            out=z_codes[:].bitcast(FP8X4),
-            scales=z_scales[:],
-            in_=z_grouped[:].rearrange("q n t -> q (n t)"),
-        )
+        quantise(z_grouped[:], z_codes[:], z_scales[:])
+        quantise_w(1)
 
         turn_w(2)
         turn_w(3)
+
+        bias_ps = sums.tile([P, OUT], BF16)
+        nc.tensor.matmul(out=bias_ps[:], lhsT=ones[:], rhs=bias_rows[:], start=True, stop=True)
         bias_sb = keep.tile([P, OUT], BF16)
-        nc.scalar.copy(out=bias_sb[:], in_=bias_ps[:])
+        nc.vector.tensor_copy(out=bias_sb[:], in_=bias_ps[:])
+
         quantise_w(2)
         quantise_w(3)
 
         z_ps = sums.tile([P, D], F32)
         nc.tensor.matmul_mx(
             out=z_ps[:],
-            lhsT=ax_codes[:, att_cols].bitcast(FP8X4),
-            lhsT_scale=ax_scales[:, att_cols],
+            lhsT=att_codes[:].bitcast(FP8X4),
+            lhsT_scale=att_scales[:],
             rhs=dic_codes[:].bitcast(FP8X4),
             rhs_scale=dic_scales[:],
             start=True,
@@ -182,14 +156,14 @@ def tile_visualdeconfounder_pb_s_kernel(tc, att_prior, dic, x, cs_w, cs_b, out_0
 
         logits_sb = keep.tile([P, OUT], F32)
         for oc in range(OUT_CHUNKS):
-            rows = slice(oc * P, (oc + 1) * P)
+            cols = slice(oc * P, (oc + 1) * P)
             logits_ps = finished.tile([P, P], F32)
             nc.tensor.matmul_mx(
                 out=logits_ps[:],
-                lhsT=ax_codes[:, x_cols].bitcast(FP8X4),
-                lhsT_scale=ax_scales[:, x_cols],
-                rhs=w_codes[:, 0, rows].bitcast(FP8X4),
-                rhs_scale=w_scales[:, 0, rows],
+                lhsT=x_codes[:].bitcast(FP8X4),
+                lhsT_scale=x_scales[:],
+                rhs=w_codes[:, oc, 0, :].bitcast(FP8X4),
+                rhs_scale=w_scales[:, oc, 0, :],
                 start=True,
                 stop=False,
             )
@@ -197,12 +171,12 @@ def tile_visualdeconfounder_pb_s_kernel(tc, att_prior, dic, x, cs_w, cs_b, out_0
                 out=logits_ps[:],
                 lhsT=z_codes[:].bitcast(FP8X4),
                 lhsT_scale=z_scales[:],
-                rhs=w_codes[:, 1, rows].bitcast(FP8X4),
-                rhs_scale=w_scales[:, 1, rows],
+                rhs=w_codes[:, oc, 1, :].bitcast(FP8X4),
+                rhs_scale=w_scales[:, oc, 1, :],
                 start=False,
                 stop=True,
             )
             nc.vector.tensor_tensor(
-                out=logits_sb[:, rows], in0=logits_ps[:], in1=bias_sb[:, rows], op=mybir.AluOpType.add
+                out=logits_sb[:, cols], in0=logits_ps[:], in1=bias_sb[:, cols], op=mybir.AluOpType.add
             )
-            nc.sync.dma_start(out=out_0[:, rows], in_=logits_sb[:, rows])
+            nc.sync.dma_start(out=out_0[:, cols], in_=logits_sb[:, cols])

@@ -17,6 +17,7 @@ OUT = 512
 W_PASSES = 2
 GROUPS = D // P
 OUT_CHUNKS = OUT // P
+CHUNKS_PER_BANK = 2
 VECTOR_GROUPS = 3
 
 FLOPS = 2 * P * K_PASS * D + 2 * P * (W_PASSES * K_PASS) * OUT
@@ -38,16 +39,16 @@ def tile_visualdeconfounder_pb_s_kernel(tc, att_prior, dic, x, cs_w, cs_b, out_0
         ones = keep.tile([P, P], BF16)
         nc.vector.memset(ones[:], 1.0)
 
-        dic_raw = keep.tile([P, PACK, D], BF16)
-        nc.sync.dma_start(
-            out=dic_raw[:].rearrange("p (u e) c -> p u e c", u=2),
-            in_=dic.rearrange("(u p e) c -> p u e c", u=2, e=2),
-        )
         att_sb = keep.tile([P, K_PASS], BF16)
         nc.sync.dma_start(out=att_sb[:], in_=att_prior)
         x_sb = keep.tile([P, K_PASS], BF16)
         nc.sync.dma_start(out=x_sb[:], in_=x)
         nc.sync.dma_start(out=bias_rows[0:1, :], in_=cs_b.unsqueeze(0))
+        dic_raw = keep.tile([P, PACK, D], BF16)
+        nc.sync.dma_start(
+            out=dic_raw[:].rearrange("p (u e) c -> p u e c", u=2),
+            in_=dic.rearrange("(u p e) c -> p u e c", u=2, e=2),
+        )
         w_sb = keep.tile([P, OUT_CHUNKS, W_PASSES * K_PASS], BF16)
         for oc in range(OUT_CHUNKS):
             nc.sync.dma_start(out=w_sb[:, oc, :], in_=cs_w[oc * P : (oc + 1) * P, :])
@@ -65,25 +66,27 @@ def tile_visualdeconfounder_pb_s_kernel(tc, att_prior, dic, x, cs_w, cs_b, out_0
                 out=codes.bitcast(FP8X4), scales=scales, in_=grouped.rearrange("p c t -> p (c t)")
             )
 
+        att_grouped = keep.tile([P, 1, P, PACK], BF16, align_bytes=64)
+        turn(att_sb[:], att_grouped[:])
+        x_grouped = keep.tile([P, 1, P, PACK], BF16, align_bytes=64)
+        turn(x_sb[:], x_grouped[:])
+        att_codes = keep.tile([P, P], U32, align_bytes=64)
+        att_scales = keep.tile([P, P], U8, align_bytes=64)
+        quantise(att_grouped[:, 0], att_codes[:], att_scales[:])
+
+        bias_ps = sums.tile([P, OUT], BF16)
+        nc.tensor.matmul(out=bias_ps[:], lhsT=ones[:], rhs=bias_rows[:], start=True, stop=True)
+
         dic_grouped = keep.tile([P, D, PACK], BF16, align_bytes=64)
         dic_sorted = dic_raw[:].rearrange("p t (u q e) -> p u e q t", u=2, e=2)
         for j in range(GROUPS):
             engine_copy = nc.vector.tensor_copy if j < VECTOR_GROUPS else nc.scalar.copy
             engine_copy(out=dic_grouped[:, j * P : (j + 1) * P, :], in_=dic_sorted[:, j // 2, j % 2])
-
-        att_grouped = keep.tile([P, 1, P, PACK], BF16, align_bytes=64)
-        turn(att_sb[:], att_grouped[:])
-        x_grouped = keep.tile([P, 1, P, PACK], BF16, align_bytes=64)
-        turn(x_sb[:], x_grouped[:])
-
         dic_codes = keep.tile([P, D], U32, align_bytes=64)
         dic_scales = keep.tile([P, D], U8, align_bytes=64)
         for j in range(GROUPS):
             cols = slice(j * P, (j + 1) * P)
             quantise(dic_grouped[:, cols, :], dic_codes[:, cols], dic_scales[:, cols])
-        att_codes = keep.tile([P, P], U32, align_bytes=64)
-        att_scales = keep.tile([P, P], U8, align_bytes=64)
-        quantise(att_grouped[:, 0], att_codes[:], att_scales[:])
 
         w_grouped = keep.tile([P, OUT_CHUNKS, W_PASSES, P, PACK], BF16, align_bytes=64)
         w_codes = keep.tile([P, OUT_CHUNKS, W_PASSES, P], U32, align_bytes=64)
@@ -118,6 +121,8 @@ def tile_visualdeconfounder_pb_s_kernel(tc, att_prior, dic, x, cs_w, cs_b, out_0
         x_codes = keep.tile([P, P], U32, align_bytes=64)
         x_scales = keep.tile([P, P], U8, align_bytes=64)
         quantise(x_grouped[:, 0], x_codes[:], x_scales[:])
+        bias_sb = keep.tile([P, OUT], BF16)
+        nc.vector.tensor_copy(out=bias_sb[:], in_=bias_ps[:])
         z_grouped = keep.tile([P, P, PACK], BF16, align_bytes=64)
         nc.vector.tensor_copy(out=z_grouped[:], in_=zt_ps[:].rearrange("q j n -> q n j"))
         quantise_w(0)
@@ -128,11 +133,6 @@ def tile_visualdeconfounder_pb_s_kernel(tc, att_prior, dic, x, cs_w, cs_b, out_0
 
         turn_w(2)
         turn_w(3)
-
-        bias_ps = sums.tile([P, OUT], BF16)
-        nc.tensor.matmul(out=bias_ps[:], lhsT=ones[:], rhs=bias_rows[:], start=True, stop=True)
-        bias_sb = keep.tile([P, OUT], BF16)
-        nc.vector.tensor_copy(out=bias_sb[:], in_=bias_ps[:])
 
         quantise_w(2)
         quantise_w(3)
@@ -155,28 +155,33 @@ def tile_visualdeconfounder_pb_s_kernel(tc, att_prior, dic, x, cs_w, cs_b, out_0
         nc.sync.dma_start(out=out_1, in_=z_sb[:])
 
         logits_sb = keep.tile([P, OUT], F32)
-        for oc in range(OUT_CHUNKS):
-            cols = slice(oc * P, (oc + 1) * P)
-            logits_ps = finished.tile([P, P], F32)
-            nc.tensor.matmul_mx(
-                out=logits_ps[:],
-                lhsT=x_codes[:].bitcast(FP8X4),
-                lhsT_scale=x_scales[:],
-                rhs=w_codes[:, oc, 0, :].bitcast(FP8X4),
-                rhs_scale=w_scales[:, oc, 0, :],
-                start=True,
-                stop=False,
-            )
-            nc.tensor.matmul_mx(
-                out=logits_ps[:],
-                lhsT=z_codes[:].bitcast(FP8X4),
-                lhsT_scale=z_scales[:],
-                rhs=w_codes[:, oc, 1, :].bitcast(FP8X4),
-                rhs_scale=w_scales[:, oc, 1, :],
-                start=False,
-                stop=True,
-            )
+        for h in range(OUT_CHUNKS // CHUNKS_PER_BANK):
+            logits_ps = finished.tile([P, CHUNKS_PER_BANK, P], F32)
+            for c in range(CHUNKS_PER_BANK):
+                oc = h * CHUNKS_PER_BANK + c
+                nc.tensor.matmul_mx(
+                    out=logits_ps[:, c, :],
+                    lhsT=x_codes[:].bitcast(FP8X4),
+                    lhsT_scale=x_scales[:],
+                    rhs=w_codes[:, oc, 0, :].bitcast(FP8X4),
+                    rhs_scale=w_scales[:, oc, 0, :],
+                    start=True,
+                    stop=False,
+                )
+                nc.tensor.matmul_mx(
+                    out=logits_ps[:, c, :],
+                    lhsT=z_codes[:].bitcast(FP8X4),
+                    lhsT_scale=z_scales[:],
+                    rhs=w_codes[:, oc, 1, :].bitcast(FP8X4),
+                    rhs_scale=w_scales[:, oc, 1, :],
+                    start=False,
+                    stop=True,
+                )
+            cols = slice(h * CHUNKS_PER_BANK * P, (h + 1) * CHUNKS_PER_BANK * P)
             nc.vector.tensor_tensor(
-                out=logits_sb[:, cols], in0=logits_ps[:], in1=bias_sb[:, cols], op=mybir.AluOpType.add
+                out=logits_sb[:, cols],
+                in0=logits_ps[:].rearrange("n c o -> n (c o)"),
+                in1=bias_sb[:, cols],
+                op=mybir.AluOpType.add,
             )
             nc.sync.dma_start(out=out_0[:, cols], in_=logits_sb[:, cols])

@@ -39,16 +39,16 @@ def tile_visualdeconfounder_pb_s_kernel(tc, att_prior, dic, x, cs_w, cs_b, out_0
         ones = keep.tile([P, P], BF16)
         nc.vector.memset(ones[:], 1.0)
 
-        att_sb = keep.tile([P, K_PASS], BF16)
-        nc.sync.dma_start(out=att_sb[:], in_=att_prior)
-        x_sb = keep.tile([P, K_PASS], BF16)
-        nc.sync.dma_start(out=x_sb[:], in_=x)
-        nc.sync.dma_start(out=bias_rows[0:1, :], in_=cs_b.unsqueeze(0))
         dic_raw = keep.tile([P, PACK, D], BF16)
         nc.sync.dma_start(
             out=dic_raw[:].rearrange("p (u e) c -> p u e c", u=2),
             in_=dic.rearrange("(u p e) c -> p u e c", u=2, e=2),
         )
+        nc.sync.dma_start(out=bias_rows[0:1, :], in_=cs_b.unsqueeze(0))
+        att_sb = keep.tile([P, K_PASS], BF16)
+        nc.sync.dma_start(out=att_sb[:], in_=att_prior)
+        x_sb = keep.tile([P, K_PASS], BF16)
+        nc.sync.dma_start(out=x_sb[:], in_=x)
         w_sb = keep.tile([P, OUT_CHUNKS, W_PASSES * K_PASS], BF16)
         for oc in range(OUT_CHUNKS):
             nc.sync.dma_start(out=w_sb[:, oc, :], in_=cs_w[oc * P : (oc + 1) * P, :])
@@ -66,14 +66,6 @@ def tile_visualdeconfounder_pb_s_kernel(tc, att_prior, dic, x, cs_w, cs_b, out_0
                 out=codes.bitcast(FP8X4), scales=scales, in_=grouped.rearrange("p c t -> p (c t)")
             )
 
-        att_grouped = keep.tile([P, 1, P, PACK], BF16, align_bytes=64)
-        turn(att_sb[:], att_grouped[:])
-        x_grouped = keep.tile([P, 1, P, PACK], BF16, align_bytes=64)
-        turn(x_sb[:], x_grouped[:])
-        att_codes = keep.tile([P, P], U32, align_bytes=64)
-        att_scales = keep.tile([P, P], U8, align_bytes=64)
-        quantise(att_grouped[:, 0], att_codes[:], att_scales[:])
-
         bias_ps = sums.tile([P, OUT], BF16)
         nc.tensor.matmul(out=bias_ps[:], lhsT=ones[:], rhs=bias_rows[:], start=True, stop=True)
 
@@ -82,11 +74,20 @@ def tile_visualdeconfounder_pb_s_kernel(tc, att_prior, dic, x, cs_w, cs_b, out_0
         for j in range(GROUPS):
             engine_copy = nc.vector.tensor_copy if j < VECTOR_GROUPS else nc.scalar.copy
             engine_copy(out=dic_grouped[:, j * P : (j + 1) * P, :], in_=dic_sorted[:, j // 2, j % 2])
+
+        att_grouped = keep.tile([P, 1, P, PACK], BF16, align_bytes=64)
+        turn(att_sb[:], att_grouped[:])
+        x_grouped = keep.tile([P, 1, P, PACK], BF16, align_bytes=64)
+        turn(x_sb[:], x_grouped[:])
+
         dic_codes = keep.tile([P, D], U32, align_bytes=64)
         dic_scales = keep.tile([P, D], U8, align_bytes=64)
         for j in range(GROUPS):
             cols = slice(j * P, (j + 1) * P)
             quantise(dic_grouped[:, cols, :], dic_codes[:, cols], dic_scales[:, cols])
+        att_codes = keep.tile([P, P], U32, align_bytes=64)
+        att_scales = keep.tile([P, P], U8, align_bytes=64)
+        quantise(att_grouped[:, 0], att_codes[:], att_scales[:])
 
         w_grouped = keep.tile([P, OUT_CHUNKS, W_PASSES, P, PACK], BF16, align_bytes=64)
         w_codes = keep.tile([P, OUT_CHUNKS, W_PASSES, P], U32, align_bytes=64)

from contextlib import ExitStack

import concourse.mybir as mybir
from concourse.masks import make_identity

BF16 = mybir.dt.bfloat16
F32 = mybir.dt.float32
U32 = mybir.dt.uint32
U8 = mybir.dt.uint8
FP8X4 = mybir.dt.float8_e4m3fn_x4

P = 128
PACK = 4
K_PASS = P * PACK
D = 512
OUT = 512
W_PASSES = 2
GROUPS = D // P
OUT_CHUNKS = OUT // P
CHUNKS_PER_BANK = 2
VECTOR_GROUPS = 3

FLOPS = 2 * P * K_PASS * D + 2 * P * (W_PASSES * K_PASS) * OUT


def tile_visualdeconfounder_pb_s_kernel(tc, att_prior, dic, x, cs_w, cs_b, out_0, out_1):
    nc = tc.nc
    with ExitStack() as ctx:
        keep = ctx.enter_context(tc.tile_pool(name="keep", bufs=1))
        turned = ctx.enter_context(tc.psum_pool(name="turned", bufs=3))
        sums = ctx.enter_context(tc.psum_pool(name="sums", bufs=1))
        finished = ctx.enter_context(tc.psum_pool(name="finished", bufs=2))
        ctx.enter_context(tc.manual_schedule())

        ident = keep.tile([P, P], F32)
        make_identity(nc, ident[:])
        bias_rows = keep.tile([P, OUT], BF16)
        nc.vector.memset(bias_rows[:], 0.0)
        ones = keep.tile([P, P], BF16)
        nc.vector.memset(ones[:], 1.0)

        dic_raw = keep.tile([P, PACK, D], BF16)
        nc.sync.dma_start(
            out=dic_raw[:].rearrange("p (u e) c -> p u e c", u=2),
            in_=dic.rearrange("(u p e) c -> p u e c", u=2, e=2),
        )
        nc.sync.dma_start(out=bias_rows[0:1, :], in_=cs_b.unsqueeze(0))
        att_sb = keep.tile([P, K_PASS], BF16)
        nc.sync.dma_start(out=att_sb[:], in_=att_prior)
        x_sb = keep.tile([P, K_PASS], BF16)
        nc.sync.dma_start(out=x_sb[:], in_=x)
        w_sb = keep.tile([P, OUT_CHUNKS, W_PASSES * K_PASS], BF16)
        for oc in range(OUT_CHUNKS):
            nc.sync.dma_start(out=w_sb[:, oc, :], in_=cs_w[oc * P : (oc + 1) * P, :])

        def turn(rows_sb, grouped):
            passes = grouped.shape[1]
            words = rows_sb.bitcast(F32)
            words_t = turned.tile([P, passes * 2, P], F32, tag="turned")
            for gu in range(passes * 2):
                nc.tensor.transpose(words_t[:, gu, :], words[:, gu * P : (gu + 1) * P], ident[:])
            nc.scalar.copy(out=grouped.bitcast(F32), in_=words_t[:].rearrange("p (g u) r -> p g r u", g=passes))

        def quantise(grouped, codes, scales):
            nc.vector.quantize_mx(
                out=codes.bitcast(FP8X4), scales=scales, in_=grouped.rearrange("p c t -> p (c t)")
            )

        bias_ps = sums.tile([P, OUT], BF16)
        nc.tensor.matmul(out=bias_ps[:], lhsT=ones[:], rhs=bias_rows[:], start=True, stop=True)

        dic_grouped = keep.tile([P, D, PACK], BF16, align_bytes=64)
        dic_sorted = dic_raw[:].rearrange("p t (u q e) -> p u e q t", u=2, e=2)
        for j in range(GROUPS):
            engine_copy = nc.vector.tensor_copy if j < VECTOR_GROUPS else nc.scalar.copy
            engine_copy(out=dic_grouped[:, j * P : (j + 1) * P, :], in_=dic_sorted[:, j // 2, j % 2])

        att_grouped = keep.tile([P, 1, P, PACK], BF16, align_bytes=64)
        turn(att_sb[:], att_grouped[:])
        x_grouped = keep.tile([P, 1, P, PACK], BF16, align_bytes=64)
        turn(x_sb[:], x_grouped[:])

        dic_codes = keep.tile([P, D], U32, align_bytes=64)
        dic_scales = keep.tile([P, D], U8, align_bytes=64)
        for j in range(GROUPS):
            cols = slice(j * P, (j + 1) * P)
            quantise(dic_grouped[:, cols, :], dic_codes[:, cols], dic_scales[:, cols])
        att_codes = keep.tile([P, P], U32, align_bytes=64)
        att_scales = keep.tile([P, P], U8, align_bytes=64)
        quantise(att_grouped[:, 0], att_codes[:], att_scales[:])

        w_grouped = keep.tile([P, OUT_CHUNKS, W_PASSES, P, PACK], BF16, align_bytes=64)
        w_codes = keep.tile([P, OUT_CHUNKS, W_PASSES, P], U32, align_bytes=64)
        w_scales = keep.tile([P, OUT_CHUNKS, W_PASSES, P], U8, align_bytes=64)

        def turn_w(oc):
            turn(w_sb[:, oc, :], w_grouped[:, oc])

        def quantise_w(oc):
            quantise(
                w_grouped[:, oc].rearrange("p g o t -> p (g o) t"),
                w_codes[:, oc].rearrange("p g o -> p (g o)"),
                w_scales[:, oc].rearrange("p g o -> p (g o)"),
            )

        turn_w(0)
        turn_w(1)

        zt_ps = sums.tile([P, GROUPS, P], F32)
        for j in range(GROUPS):
            cols = slice(j * P, (j + 1) * P)
            nc.tensor.matmul_mx(
                out=zt_ps[:, j, :],
                lhsT=dic_codes[:, cols].bitcast(FP8X4),
                lhsT_scale=dic_scales[:, cols],
                rhs=att_codes[:].bitcast(FP8X4),
                rhs_scale=att_scales[:],
                start=True,
                stop=True,
            )

        x_codes = keep.tile([P, P], U32, align_bytes=64)
        x_scales = keep.tile([P, P], U8, align_bytes=64)
        quantise(x_grouped[:, 0], x_codes[:], x_scales[:])
        bias_sb = keep.tile([P, OUT], BF16)
        nc.vector.tensor_copy(out=bias_sb[:], in_=bias_ps[:])
        z_grouped = keep.tile([P, P, PACK], BF16, align_bytes=64)
        nc.vector.tensor_copy(out=z_grouped[:], in_=zt_ps[:].rearrange("q j n -> q n j"))
        quantise_w(0)
        z_codes = keep.tile([P, P], U32, align_bytes=64)
        z_scales = keep.tile([P, P], U8, align_bytes=64)
        quantise(z_grouped[:], z_codes[:], z_scales[:])
        quantise_w(1)

        turn_w(2)
        turn_w(3)

        quantise_w(2)
        quantise_w(3)

        z_ps = sums.tile([P, D], F32)
        nc.tensor.matmul_mx(
            out=z_ps[:],
            lhsT=att_codes[:].bitcast(FP8X4),
            lhsT_scale=att_scales[:],
            rhs=dic_codes[:].bitcast(FP8X4),
            rhs_scale=dic_scales[:],
            start=True,
            stop=True,
        )
        z_sb = keep.tile([P, D], F32)
        nc.scalar.copy(
            out=z_sb[:].rearrange("n (u q e) -> n u q e", u=2, e=2),
            in_=z_ps[:].rearrange("n (u e q) -> n u q e", u=2, e=2),
        )
        nc.sync.dma_start(out=out_1, in_=z_sb[:])

        logits_sb = keep.tile([P, OUT], F32)
        for h in range(OUT_CHUNKS // CHUNKS_PER_BANK):
            logits_ps = finished.tile([P, CHUNKS_PER_BANK, P], F32)
            for c in range(CHUNKS_PER_BANK):
                oc = h * CHUNKS_PER_BANK + c
                nc.tensor.matmul_mx(
                    out=logits_ps[:, c, :],
                    lhsT=x_codes[:].bitcast(FP8X4),
                    lhsT_scale=x_scales[:],
                    rhs=w_codes[:, oc, 0, :].bitcast(FP8X4),
                    rhs_scale=w_scales[:, oc, 0, :],
                    start=True,
                    stop=False,
                )
                nc.tensor.matmul_mx(
                    out=logits_ps[:, c, :],
                    lhsT=z_codes[:].bitcast(FP8X4),
                    lhsT_scale=z_scales[:],
                    rhs=w_codes[:, oc, 1, :].bitcast(FP8X4),
                    rhs_scale=w_scales[:, oc, 1, :],
                    start=False,
                    stop=True,
                )
            cols = slice(h * CHUNKS_PER_BANK * P, (h + 1) * CHUNKS_PER_BANK * P)
            nc.vector.tensor_tensor(
                out=logits_sb[:, cols],
                in0=logits_ps[:].rearrange("n c o -> n (c o)"),
                in1=bias_sb[:, cols],
                op=mybir.AluOpType.add,
            )
            nc.sync.dma_start(out=out_0[:, cols], in_=logits_sb[:, cols])
